import numpy as np
import ml_dtypes


def mxq(x, axis, fmt="e4m3"):
    dtype, down = {"e4m3": (ml_dtypes.float8_e4m3fn, 7), "e5m2": (ml_dtypes.float8_e5m2, 14)}[fmt]
    v = np.moveaxis(np.asarray(x, np.float32).astype(ml_dtypes.bfloat16).astype(np.float64), axis, -1)
    blocks = v.reshape(v.shape[:-1] + (-1, 32))
    amax = np.abs(blocks).max(-1, keepdims=True)
    byte = np.maximum(np.where(amax > 0, np.frexp(amax)[1] - 1 + 127, 0) - down, 1)
    scale = np.exp2(byte - 127.0)
    codes = (blocks / scale).astype(np.float32).astype(dtype).astype(np.float64)
    return np.moveaxis((codes * scale).reshape(v.shape), -1, axis)


WIDE = False


def mx_kscale(k):
    if not WIDE:
        return np.ones(k)
    levels = np.array([10, -10, 5, -5, 0])
    if k % 512:
        return np.exp2(np.random.permutation(np.resize(levels, k // 32))).repeat(32)
    a = np.empty((k // 512, 16))
    for p in range(k // 512):
        a[p, :8] = np.random.permutation(np.resize(levels, 8))
        for g in range(8):
            far = levels[np.abs(levels - a[p, g]) >= 10]
            a[p, g + 8] = far[np.random.randint(len(far))]
    return np.exp2(a.ravel()).repeat(32)


BF16 = ml_dtypes.bfloat16


def bf(x):
    return np.asarray(x, np.float32).astype(BF16)


def f64(x):
    return np.asarray(x).astype(np.float64)


B, S, D_IN, D_MODEL = 8, 512, 1024, 512


def relu(v):
    return np.maximum(v, 0.0)


def setup_inputs():
    s = mx_kscale(D_MODEL)
    t = mx_kscale(S)
    return {"qp": bf(np.random.standard_normal((B, S, D_MODEL)) * 0.4 * s),
            "kp": bf(np.random.standard_normal((B, S, D_MODEL)) * 0.4 / s * t[:, None]),
            "vp": bf(np.random.standard_normal((B, S, D_MODEL)) * 0.25 / t[:, None]),
            "mask": bf(np.random.standard_normal((1, S, S)) * 0.1 * t)}


def reference(qp, kp, vp, mask):
    scores = relu(mxq(f64(qp), 2, "e4m3") @ mxq(f64(kp), 2, "e4m3").transpose(0, 2, 1))
    logits = scores / np.sqrt(D_MODEL) + f64(mask)
    return relu(mxq(logits, 2, "e4m3") @ mxq(f64(vp), 1, "e4m3"))

@@ -1,0 +1,352 @@
+import math
+from contextlib import ExitStack
+
+import concourse.mybir as mybir
+from concourse.masks import make_identity
+
+F32 = mybir.dt.float32
+BF16 = mybir.dt.bfloat16
+U32 = mybir.dt.uint32
+U8 = mybir.dt.uint8
+FP8X4 = mybir.dt.float8_e4m3fn_x4
+ALU = mybir.AluOpType
+ACT = mybir.ActivationFunctionType
+
+NB = 8
+S = 512
+D = 512
+P = 128
+FLOPS = 2 * 2 * NB * S * S * D
+
+INV_SQRT_D = 1.0 / math.sqrt(D)
+R_GPSIMD_GROUPS = 48
+MANUAL = True
+SCALAR_TAIL = 6
+
+
+def tile_scaledconvolutionaldotproduct_pa_t_kernel(tc, qp, kp, vp, mask, out):
+    nc = tc.nc
+    with ExitStack() as ctx:
+        if MANUAL:
+            ctx.enter_context(tc.manual_schedule())
+        const = ctx.enter_context(tc.tile_pool(name="const", bufs=1))
+        raw = ctx.enter_context(tc.tile_pool(name="raw", bufs=NB))
+        work = ctx.enter_context(tc.tile_pool(name="work", bufs=2))
+        ps_t = ctx.enter_context(tc.psum_pool(name="ps_t", bufs=3))
+        ps_1 = ctx.enter_context(tc.psum_pool(name="ps_1", bufs=3))
+        ps_2 = ctx.enter_context(tc.psum_pool(name="ps_2", bufs=2))
+
+        ident = const.tile([P, P], F32)
+        make_identity(nc, ident[:])
+        m_sb = const.tile([P, 4 * S], BF16)
+        mask_g = const.tile([P, 4 * S], BF16, align_bytes=64)
+
+        st = {}
+
+        def live(b):
+            return 0 <= b < NB
+
+        def rows(x):
+            return x.rearrange("(p j) d -> p (j d)", j=4)
+
+        def load(b):
+            k_sb = raw.tile([P, 4 * D], BF16)
+            q_sb = raw.tile([P, 4 * D], BF16)
+            v_sb = raw.tile([P, 4 * D], BF16)
+            if b == 0:
+                for x_sb, x, h in (
+                    (k_sb, kp[0], 0),
+                    (k_sb, kp[0], 1),
+                    (q_sb, qp[0], 0),
+                    (m_sb, mask[0], 0),
+                    (q_sb, qp[0], 1),
+                    (m_sb, mask[0], 1),
+                ):
+                    half = slice(2 * D * h, 2 * D * (h + 1))
+                    nc.sync.dma_start(out=x_sb[:, half], in_=rows(x)[:, half])
+            else:
+                nc.sync.dma_start(out=k_sb[:], in_=rows(kp[b]))
+                nc.sync.dma_start(out=q_sb[:], in_=rows(qp[b]))
+            nc.sync.dma_start(out=v_sb[:], in_=rows(vp[b]))
+            st[("raw", b)] = (k_sb, q_sb, v_sb)
+
+        def copy_out(engine, dst, src):
+            if engine == "s":
+                nc.scalar.copy(out=dst, in_=src)
+            else:
+                nc.vector.tensor_copy(out=dst, in_=src)
+
+        def unpack(engine, g32, n, tp):
+            copy_out(
+                engine,
+                g32[:, 512 * n : 512 * (n + 1)].rearrange("p (j r u) -> p j r u", j=2, u=2),
+                tp[:].rearrange("p j u r -> p j r u"),
+            )
+
+        def mask_transposes(h):
+            m32 = m_sb[:].bitcast(F32).rearrange("r (j p u) -> r j p u", j=4, u=2)
+            tp = ps_2.tile([P, 2, 2, P], F32, tag="s2")
+            for jj in range(2):
+                for u in range(2):
+                    nc.tensor.transpose(tp[:, jj, u, :], m32[:, 2 * h + jj, :, u], ident[:])
+            st[("mt", h)] = tp
+
+        def mask_copy(h):
+            unpack("s", mask_g[:].bitcast(F32), h, st[("mt", h)])
+
+        def transposes(b, n):
+            if not live(b):
+                return
+            if n == 0:
+                qk_g = work.tile([P, 8 * S], BF16, align_bytes=64)
+                st[("qkg", b)] = qk_g
+            s32 = st[("raw", b)][n // 2][:].bitcast(F32)
+            tp = ps_t.tile([P, 2, 2, P], F32, tag="tp")
+            for jj in range(2):
+                for u in range(2):
+                    c0 = (2 * (n % 2) + jj) * 256 + u
+                    nc.tensor.transpose(tp[:, jj, u, :], s32[:, c0 : c0 + 255 : 2], ident[:])
+            st[("tp", b, n)] = tp
+
+        def copy(b, n, engine):
+            if not live(b):
+                return
+            unpack(engine, st[("qkg", b)][:].bitcast(F32), n, st[("tp", b, n)])
+
+        def quantise_qk(b, lo, hi):
+            if not live(b):
+                return
+            if lo == 0:
+                qk_c = work.tile([P, 2 * S], U32, align_bytes=64)
+                qk_s = work.tile([P, 2 * S], U8, align_bytes=64)
+                st[("qk", b)] = (qk_c, qk_s)
+            qk_g = st[("qkg", b)]
+            qk_c, qk_s = st[("qk", b)]
+            w = slice(2 * P * lo, 2 * P * hi)
+            nc.vector.quantize_mx(
+                out=qk_c[:, w].bitcast(FP8X4),
+                scales=qk_s[:, w],
+                in_=qk_g[:, 8 * P * lo : 8 * P * hi],
+            )
+
+        def scores(b, j):
+            if not live(b):
+                return
+            qk_c, qk_s = st[("qk", b)]
+            if ("s1", b, j) not in st:
+                s1 = ps_1.tile([P, 4, P], F32, tag="s1")
+                st[("s1", b, j)] = s1
+            s1 = st[("s1", b, j)]
+            for t in range(4):
+                kc = slice(P * t, P * (t + 1))
+                qc = slice(S + P * j, S + P * (j + 1))
+                nc.tensor.matmul_mx(
+                    out=s1[:, t, :],
+                    lhsT=qk_c[:, kc].bitcast(FP8X4),
+                    lhsT_scale=qk_s[:, kc],
+                    rhs=qk_c[:, qc].bitcast(FP8X4),
+                    rhs_scale=qk_s[:, qc],
+                    start=True,
+                    stop=True,
+                )
+
+        def logits(b, j):
+            if not live(b):
+                return
+            cols = slice(4 * P * j, 4 * P * (j + 1))
+            if b >= SCALAR_TAIL:
+                if j == 0:
+                    l_g = work.tile([P, 4 * S], BF16, align_bytes=64)
+                    st[("l", b)] = l_g
+                a = work.tile([P, P, 4], F32, bufs=3)
+                nc.scalar.activation(
+                    out=a[:],
+                    in_=st[("s1", b, j)][:].rearrange("p t r -> p r t"),
+                    func=ACT.Relu,
+                    scale=INV_SQRT_D,
+                )
+                nc.vector.tensor_tensor(
+                    out=st[("l", b)][:, cols],
+                    in0=a[:].rearrange("p r t -> p (r t)"),
+                    in1=mask_g[:, cols],
+                    op=ALU.add,
+                )
+                return
+            if j == 0:
+                x_g = work.tile([P, 4 * S], BF16, align_bytes=64)
+                st[("x", b)] = x_g
+            x_g = st[("x", b)]
+            nc.vector.scalar_tensor_tensor(
+                out=x_g[:, cols].rearrange("p (r t) -> p r t", t=4),
+                in0=st[("s1", b, j)][:].rearrange("p t r -> p r t"),
+                scalar=INV_SQRT_D,
+                in1=mask_g[:, cols].rearrange("p (r t) -> p r t", t=4),
+                op0=ALU.mult,
+                op1=ALU.add,
+            )
+
+        def clamp(b):
+            if not live(b) or b >= SCALAR_TAIL:
+                return
+            l_g = work.tile([P, 4 * S], BF16, align_bytes=64)
+            nc.vector.tensor_tensor(out=l_g[:], in0=st[("x", b)][:], in1=mask_g[:], op=ALU.max)
+            st[("l", b)] = l_g
+
+        def quantise_l(b, lo, hi):
+            if not live(b):
+                return
+            if lo == 0:
+                l_c = work.tile([P, S], U32, align_bytes=64)
+                l_s = work.tile([P, S], U8, align_bytes=64)
+                st[("lc", b)] = (l_c, l_s)
+            l_c, l_s = st[("lc", b)]
+            w = slice(P * lo, P * hi)
+            nc.vector.quantize_mx(
+                out=l_c[:, w].bitcast(FP8X4),
+                scales=l_s[:, w],
+                in_=st[("l", b)][:, 4 * P * lo : 4 * P * hi],
+            )
+
+        def regroup(b, engine, lo, hi):
+            if not live(b) or lo == hi:
+                return
+            if ("vg", b) not in st:
+                v_g = work.tile([P, 4 * D], BF16, align_bytes=64)
+                st[("vg", b)] = v_g
+            dst = st[("vg", b)][:].rearrange("p (c i t) -> p c t i", i=4, t=4)[:, lo:hi]
+            src = st[("raw", b)][2][:].rearrange("p (t c i) -> p c t i", i=4, t=4)[:, lo:hi]
+            if engine == "g":
+                nc.gpsimd.tensor_scalar(
+                    out=dst, in0=src, scalar1=1.0, scalar2=0.0, op0=ALU.mult, op1=ALU.add
+                )
+            else:
+                copy_out(engine, dst, src)
+
+        def quantise_v(b):
+            if not live(b):
+                return
+            v_c = work.tile([P, D], U32, align_bytes=64)
+            v_s = work.tile([P, D], U8, align_bytes=64)
+            nc.vector.quantize_mx(out=v_c[:].bitcast(FP8X4), scales=v_s[:], in_=st[("vg", b)][:])
+            st[("vc", b)] = (v_c, v_s)
+
+        def product(b, j, spare=False):
+            if not live(b):
+                return
+            l_c, l_s = st[("lc", b)]
+            v_c, v_s = st[("vc", b)]
+            if spare:
+                s2 = ps_t.tile([P, D], F32, tag="tp")
+            else:
+                s2 = ps_2.tile([P, D], F32, tag="s2")
+            qc = slice(P * j, P * (j + 1))
+            nc.tensor.matmul_mx(
+                out=s2[:],
+                lhsT=l_c[:, qc].bitcast(FP8X4),
+                lhsT_scale=l_s[:, qc],
+                rhs=v_c[:].bitcast(FP8X4),
+                rhs_scale=v_s[:],
+                start=True,
+                stop=True,
+            )
+            st[("s2", b, j)] = s2
+
+        def result(b, j, engine):
+            if not live(b):
+                return
+            if j == 0:
+                o_sb = work.tile([P, 4 * D], F32, bufs=5)
+                st[("o", b)] = o_sb
+            dst = st[("o", b)][:, D * j : D * (j + 1)]
+            if engine == "s":
+                nc.scalar.activation(out=dst, in_=st[("s2", b, j)][:], func=ACT.Relu)
+            else:
+                nc.vector.tensor_scalar_max(out=dst, in0=st[("s2", b, j)][:], scalar1=0.0)
+
+        def store(b, lo, hi):
+            if not live(b):
+                return
+            part = slice(D * lo, D * hi)
+            nc.sync.dma_start(out=rows(out[b])[:, part], in_=st[("o", b)][:, part])
+
+        for b in range(NB):
+            load(b)
+
+        for n in range(3):
+            transposes(0, n)
+        copy(0, 0, "s")
+        copy(0, 1, "v")
+        mask_transposes(0)
+        quantise_qk(0, 0, 2)
+        copy(0, 2, "s")
+        transposes(0, 3)
+        mask_copy(0)
+        quantise_qk(0, 2, 3)
+        scores(0, 0)
+        scores(0, 1)
+        mask_transposes(1)
+        copy(0, 3, "s")
+        mask_copy(1)
+        regroup(0, "g", 0, P // 2)
+        regroup(0, "g", P // 2, P)
+
+        last = NB - 1
+        for c in range(NB):
+            split = 0 if c + 1 == last else R_GPSIMD_GROUPS
+            regroup(c + 1, "g", 0, split)
+            logits(c, 0)
+            if c == 0:
+                quantise_qk(0, 3, 4)
+                scores(0, 2)
+            scores(c, 3)
+            logits(c, 1)
+            if c == 0:
+                for n in range(3):
+                    transposes(1, n)
+                copy(1, 0, "s")
+                transposes(1, 3)
+                for n in range(1, 4):
+                    copy(1, n, "s")
+            if c == last:
+                quantise_l(c, 0, 2)
+                product(c, 0, spare=True)
+                product(c, 1, spare=True)
+            result(c - 1, 0, "s")
+            product(c - 1, 2)
+            result(c - 1, 1, "s")
+            product(c - 1, 3)
+            logits(c, 2)
+            logits(c, 3)
+            regroup(c + 1, "s", split, P)
+            if c != last:
+                for n in range(3):
+                    transposes(c + 2, n)
+                copy(c + 2, 0, "s")
+                transposes(c + 2, 3)
+            result(c - 1, 2, "s")
+            result(c - 1, 3, "s")
+            store(c - 1, 0, 4)
+            if c == last:
+                quantise_l(c, 2, 4)
+                product(c, 2)
+                product(c, 3)
+                result(c, 0, "s")
+                result(c, 1, "v")
+                store(c, 0, 2)
+                result(c, 2, "s")
+                store(c, 2, 3)
+                result(c, 3, "v")
+                store(c, 3, 4)
+                break
+            for n in range(1, 4):
+                copy(c + 2, n, "s")
+            clamp(c)
+            quantise_qk(c + 1, 0, 4)
+            for j in range(3):
+                scores(c + 1, j)
+            quantise_l(c, 0, 4)
+            quantise_v(c)
+            if c + 1 == last:
+                quantise_v(last)
+            product(c, 0)
+            product(c, 1)

@@ -19,7 +19,7 @@ P = 128
 FLOPS = 2 * 2 * NB * S * S * D
 
 INV_SQRT_D = 1.0 / math.sqrt(D)
-R_GPSIMD_GROUPS = 48
+R_GPSIMD_GROUPS = 112
 MANUAL = True
 SCALAR_TAIL = 6
 

@@ -340,12 +340,12 @@ def tile_scaledconvolutionaldotproduct_pa_t_kernel(tc, qp, kp, vp, mask, out):
                 break
             for n in range(1, 4):
                 copy(c + 2, n, "s")
-            clamp(c)
             quantise_qk(c + 1, 0, 4)
             for j in range(3):
                 scores(c + 1, j)
-            quantise_l(c, 0, 4)
+            clamp(c)
             quantise_v(c)
+            quantise_l(c, 0, 4)
             if c + 1 == last:
                 quantise_v(last)
             product(c, 0)

@@ -19,16 +19,15 @@ P = 128
 FLOPS = 2 * 2 * NB * S * S * D
 
 INV_SQRT_D = 1.0 / math.sqrt(D)
-R_GPSIMD_GROUPS = 112
-MANUAL = True
-SCALAR_TAIL = 6
+RELU_BANKS = (0, 0, 0, 0, 0, 0, 0, 4)
+G_GROUPS = 104
+V_LAST_FROM = 3
 
 
 def tile_scaledconvolutionaldotproduct_pa_t_kernel(tc, qp, kp, vp, mask, out):
     nc = tc.nc
     with ExitStack() as ctx:
-        if MANUAL:
-            ctx.enter_context(tc.manual_schedule())
+        ctx.enter_context(tc.manual_schedule())
         const = ctx.enter_context(tc.tile_pool(name="const", bufs=1))
         raw = ctx.enter_context(tc.tile_pool(name="raw", bufs=NB))
         work = ctx.enter_context(tc.tile_pool(name="work", bufs=2))
@@ -49,26 +48,23 @@ def tile_scaledconvolutionaldotproduct_pa_t_kernel(tc, qp, kp, vp, mask, out):
         def rows(x):
             return x.rearrange("(p j) d -> p (j d)", j=4)
 
-        def load(b):
+        def load_kq(b):
             k_sb = raw.tile([P, 4 * D], BF16)
             q_sb = raw.tile([P, 4 * D], BF16)
-            v_sb = raw.tile([P, 4 * D], BF16)
             if b == 0:
-                for x_sb, x, h in (
-                    (k_sb, kp[0], 0),
-                    (k_sb, kp[0], 1),
-                    (q_sb, qp[0], 0),
-                    (m_sb, mask[0], 0),
-                    (q_sb, qp[0], 1),
-                    (m_sb, mask[0], 1),
-                ):
-                    half = slice(2 * D * h, 2 * D * (h + 1))
-                    nc.sync.dma_start(out=x_sb[:, half], in_=rows(x)[:, half])
+                for x_sb, x in ((k_sb, kp[0]), (q_sb, qp[0]), (m_sb, mask[0])):
+                    for h in range(2):
+                        half = slice(2 * D * h, 2 * D * (h + 1))
+                        nc.sync.dma_start(out=x_sb[:, half], in_=rows(x)[:, half])
             else:
                 nc.sync.dma_start(out=k_sb[:], in_=rows(kp[b]))
                 nc.sync.dma_start(out=q_sb[:], in_=rows(qp[b]))
+            st[("raw", b)] = (k_sb, q_sb)
+
+        def load_v(b):
+            v_sb = raw.tile([P, 4 * D], BF16)
             nc.sync.dma_start(out=v_sb[:], in_=rows(vp[b]))
-            st[("raw", b)] = (k_sb, q_sb, v_sb)
+            st[("v", b)] = v_sb
 
         def copy_out(engine, dst, src):
             if engine == "s":
@@ -91,8 +87,8 @@ def tile_scaledconvolutionaldotproduct_pa_t_kernel(tc, qp, kp, vp, mask, out):
                     nc.tensor.transpose(tp[:, jj, u, :], m32[:, 2 * h + jj, :, u], ident[:])
             st[("mt", h)] = tp
 
-        def mask_copy(h):
-            unpack("s", mask_g[:].bitcast(F32), h, st[("mt", h)])
+        def mask_copy(h, engine):
+            unpack(engine, mask_g[:].bitcast(F32), h, st[("mt", h)])
 
         def transposes(b, n):
             if not live(b):
@@ -101,7 +97,10 @@ def tile_scaledconvolutionaldotproduct_pa_t_kernel(tc, qp, kp, vp, mask, out):
                 qk_g = work.tile([P, 8 * S], BF16, align_bytes=64)
                 st[("qkg", b)] = qk_g
             s32 = st[("raw", b)][n // 2][:].bitcast(F32)
-            tp = ps_t.tile([P, 2, 2, P], F32, tag="tp")
+            if b == 0 and n == 3:
+                tp = ps_1.tile([P, 2, 2, P], F32, tag="s1")
+            else:
+                tp = ps_t.tile([P, 2, 2, P], F32, tag="tp")
             for jj in range(2):
                 for u in range(2):
                     c0 = (2 * (n % 2) + jj) * 256 + u
@@ -150,24 +149,30 @@ def tile_scaledconvolutionaldotproduct_pa_t_kernel(tc, qp, kp, vp, mask, out):
                     stop=True,
                 )
 
+        def relu(b, j):
+            a = work.tile([P, P, 4], F32, bufs=4)
+            nc.scalar.activation(
+                out=a[:],
+                in_=st[("s1", b, j)][:].rearrange("p t r -> p r t"),
+                func=ACT.Relu,
+                scale=INV_SQRT_D,
+            )
+            st[("a", b, j)] = a
+
+        def relu_banks(b):
+            return RELU_BANKS[b] if live(b) else 0
+
         def logits(b, j):
             if not live(b):
                 return
             cols = slice(4 * P * j, 4 * P * (j + 1))
-            if b >= SCALAR_TAIL:
-                if j == 0:
-                    l_g = work.tile([P, 4 * S], BF16, align_bytes=64)
-                    st[("l", b)] = l_g
-                a = work.tile([P, P, 4], F32, bufs=3)
-                nc.scalar.activation(
-                    out=a[:],
-                    in_=st[("s1", b, j)][:].rearrange("p t r -> p r t"),
-                    func=ACT.Relu,
-                    scale=INV_SQRT_D,
-                )
+            if j == 0:
+                l_g = work.tile([P, 4 * S], BF16, align_bytes=64)
+                st[("l", b)] = l_g
+            if j >= 4 - RELU_BANKS[b]:
                 nc.vector.tensor_tensor(
                     out=st[("l", b)][:, cols],
-                    in0=a[:].rearrange("p r t -> p (r t)"),
+                    in0=st[("a", b, j)][:].rearrange("p r t -> p (r t)"),
                     in1=mask_g[:, cols],
                     op=ALU.add,
                 )
@@ -186,11 +191,12 @@ def tile_scaledconvolutionaldotproduct_pa_t_kernel(tc, qp, kp, vp, mask, out):
             )
 
         def clamp(b):
-            if not live(b) or b >= SCALAR_TAIL:
+            if not live(b) or RELU_BANKS[b] == 4:
                 return
-            l_g = work.tile([P, 4 * S], BF16, align_bytes=64)
-            nc.vector.tensor_tensor(out=l_g[:], in0=st[("x", b)][:], in1=mask_g[:], op=ALU.max)
-            st[("l", b)] = l_g
+            rest = slice(0, 4 * P * (4 - RELU_BANKS[b]))
+            nc.vector.tensor_tensor(
+                out=st[("l", b)][:, rest], in0=st[("x", b)][:, rest], in1=mask_g[:, rest], op=ALU.max
+            )
 
         def quantise_l(b, lo, hi):
             if not live(b):
@@ -211,10 +217,14 @@ def tile_scaledconvolutionaldotproduct_pa_t_kernel(tc, qp, kp, vp, mask, out):
             if not live(b) or lo == hi:
                 return
             if ("vg", b) not in st:
-                v_g = work.tile([P, 4 * D], BF16, align_bytes=64)
-                st[("vg", b)] = v_g
+                if b == NB - 1:
+                    v_last = const.tile([P, 4 * D], BF16, align_bytes=64)
+                    st[("vg", b)] = v_last
+                else:
+                    v_g = const.tile([P, 4 * D], BF16, align_bytes=64)
+                    st[("vg", b)] = v_g
             dst = st[("vg", b)][:].rearrange("p (c i t) -> p c t i", i=4, t=4)[:, lo:hi]
-            src = st[("raw", b)][2][:].rearrange("p (t c i) -> p c t i", i=4, t=4)[:, lo:hi]
+            src = st[("v", b)][:].rearrange("p (t c i) -> p c t i", i=4, t=4)[:, lo:hi]
             if engine == "g":
                 nc.gpsimd.tensor_scalar(
                     out=dst, in0=src, scalar1=1.0, scalar2=0.0, op0=ALU.mult, op1=ALU.add
@@ -230,13 +240,15 @@ def tile_scaledconvolutionaldotproduct_pa_t_kernel(tc, qp, kp, vp, mask, out):
             nc.vector.quantize_mx(out=v_c[:].bitcast(FP8X4), scales=v_s[:], in_=st[("vg", b)][:])
             st[("vc", b)] = (v_c, v_s)
 
-        def product(b, j, spare=False):
+        def product(b, j, bank="2"):
             if not live(b):
                 return
             l_c, l_s = st[("lc", b)]
             v_c, v_s = st[("vc", b)]
-            if spare:
+            if bank == "t":
                 s2 = ps_t.tile([P, D], F32, tag="tp")
+            elif bank == "1":
+                s2 = ps_1.tile([P, D], F32, tag="s1")
             else:
                 s2 = ps_2.tile([P, D], F32, tag="s2")
             qc = slice(P * j, P * (j + 1))
@@ -269,81 +281,94 @@ def tile_scaledconvolutionaldotproduct_pa_t_kernel(tc, qp, kp, vp, mask, out):
             part = slice(D * lo, D * hi)
             nc.sync.dma_start(out=rows(out[b])[:, part], in_=st[("o", b)][:, part])
 
-        for b in range(NB):
-            load(b)
+        load_kq(0)
+        for b in range(1, NB):
+            load_v(b - 1)
+            load_kq(b)
+        load_v(NB - 1)
 
-        for n in range(3):
+        for n in range(4):
             transposes(0, n)
-        copy(0, 0, "s")
-        copy(0, 1, "v")
+        copy(0, 0, "v")
+        copy(0, 1, "s")
         mask_transposes(0)
-        quantise_qk(0, 0, 2)
+        mask_transposes(1)
         copy(0, 2, "s")
-        transposes(0, 3)
-        mask_copy(0)
+        quantise_qk(0, 0, 2)
+        copy(0, 3, "s")
         quantise_qk(0, 2, 3)
         scores(0, 0)
         scores(0, 1)
-        mask_transposes(1)
-        copy(0, 3, "s")
-        mask_copy(1)
-        regroup(0, "g", 0, P // 2)
-        regroup(0, "g", P // 2, P)
+        mask_copy(0, "v")
+        quantise_qk(0, 3, 4)
+        scores(0, 2)
+        mask_copy(1, "s")
 
         last = NB - 1
         for c in range(NB):
-            split = 0 if c + 1 == last else R_GPSIMD_GROUPS
-            regroup(c + 1, "g", 0, split)
+            if c < last:
+                regroup(c, "g", 0, G_GROUPS)
             logits(c, 0)
-            if c == 0:
-                quantise_qk(0, 3, 4)
-                scores(0, 2)
-            scores(c, 3)
+            if relu_banks(c) < 4:
+                scores(c, 3)
+                for j in range(4 - relu_banks(c), 4):
+                    relu(c, j)
             logits(c, 1)
             if c == 0:
-                for n in range(3):
+                for n in range(4):
                     transposes(1, n)
-                copy(1, 0, "s")
-                transposes(1, 3)
-                for n in range(1, 4):
                     copy(1, n, "s")
+            if c < last:
+                regroup(c, "s", G_GROUPS, P)
+            transposes(c + 2, 0)
+            transposes(c + 2, 1)
+            result(c - 1, 0, "s")
+            product(c - 1, 2, "t" if c == last else "2")
+            result(c - 1, 1, "s")
+            product(c - 1, 3, "t" if c == last else "2")
             if c == last:
                 quantise_l(c, 0, 2)
-                product(c, 0, spare=True)
-                product(c, 1, spare=True)
-            result(c - 1, 0, "s")
-            product(c - 1, 2)
-            result(c - 1, 1, "s")
-            product(c - 1, 3)
+                product(c, 0, "1")
+                product(c, 1, "1")
             logits(c, 2)
             logits(c, 3)
-            regroup(c + 1, "s", split, P)
-            if c != last:
-                for n in range(3):
-                    transposes(c + 2, n)
-                copy(c + 2, 0, "s")
-                transposes(c + 2, 3)
+            copy(c + 2, 0, "s")
+            copy(c + 2, 1, "s")
             result(c - 1, 2, "s")
+            store(c - 1, 0, 2)
             result(c - 1, 3, "s")
-            store(c - 1, 0, 4)
+            store(c - 1, 2, 4)
             if c == last:
                 quantise_l(c, 2, 4)
                 product(c, 2)
                 product(c, 3)
                 result(c, 0, "s")
+                store(c, 0, 1)
                 result(c, 1, "v")
-                store(c, 0, 2)
+                store(c, 1, 2)
                 result(c, 2, "s")
                 store(c, 2, 3)
                 result(c, 3, "v")
                 store(c, 3, 4)
                 break
-            for n in range(1, 4):
-                copy(c + 2, n, "s")
+            if c >= V_LAST_FROM:
+                piece = P // (last - V_LAST_FROM)
+                regroup(last, "s", piece * (c - V_LAST_FROM), piece * (c + 1 - V_LAST_FROM))
+            if c == 0:
+                clamp(c)
             quantise_qk(c + 1, 0, 4)
             for j in range(3):
                 scores(c + 1, j)
-            clamp(c)
+            if relu_banks(c + 1) == 4:
+                for j in range(3):
+                    relu(c + 1, j)
+                scores(c + 1, 3)
+                relu(c + 1, 3)
+            for n in (2, 3):
+                transposes(c + 2, n)
+                copy(c + 2, n, "s")
+            if c != 0:
+                clamp(c)
             quantise_v(c)
             quantise_l(c, 0, 4)
             if c + 1 == last:

@@ -232,6 +232,11 @@ def tile_scaledconvolutionaldotproduct_pa_t_kernel(tc, qp, kp, vp, mask, out):
             else:
                 copy_out(engine, dst, src)
 
+        def gate_regroup(b):
+            v_g = const.tile([P, 4 * D], BF16, align_bytes=64)
+            st[("vg", b)] = v_g
+            nc.vector.memset(v_g[:, :2], 0.0)
+
         def quantise_v(b):
             if not live(b):
                 return
@@ -292,15 +297,16 @@ def tile_scaledconvolutionaldotproduct_pa_t_kernel(tc, qp, kp, vp, mask, out):
         copy(0, 0, "v")
         copy(0, 1, "s")
         mask_transposes(0)
-        mask_transposes(1)
         copy(0, 2, "s")
         quantise_qk(0, 0, 2)
         copy(0, 3, "s")
         quantise_qk(0, 2, 3)
         scores(0, 0)
         scores(0, 1)
+        mask_transposes(1)
         mask_copy(0, "v")
         quantise_qk(0, 3, 4)
+        gate_regroup(0)
         scores(0, 2)
         mask_copy(1, "s")
 

@@ -328,25 +328,36 @@ def tile_scaledconvolutionaldotproduct_pa_t_kernel(tc, qp, kp, vp, mask, out):
                 regroup(c, "s", G_GROUPS, P)
             transposes(c + 2, 0)
             transposes(c + 2, 1)
+            if c == 0:
+                transposes(c + 2, 2)
             result(c - 1, 0, "s")
             product(c - 1, 2, "t" if c == last else "2")
             result(c - 1, 1, "s")
+            if c == last:
+                relu(c, 3)
             product(c - 1, 3, "t" if c == last else "2")
+            logits(c, 2)
             if c == last:
                 quantise_l(c, 0, 2)
                 product(c, 0, "1")
                 product(c, 1, "1")
-            logits(c, 2)
             logits(c, 3)
             copy(c + 2, 0, "s")
             copy(c + 2, 1, "s")
-            result(c - 1, 2, "s")
-            store(c - 1, 0, 2)
-            result(c - 1, 3, "s")
-            store(c - 1, 2, 4)
             if c == last:
-                quantise_l(c, 2, 4)
+                store(c - 1, 0, 1)
+                store(c - 1, 1, 2)
+            result(c - 1, 2, "s")
+            if c == last:
+                store(c - 1, 2, 3)
+            else:
+                store(c - 1, 0, 2)
+            result(c - 1, 3, "s")
+            store(c - 1, 3 if c == last else 2, 4)
+            if c == last:
+                quantise_l(c, 2, 3)
                 product(c, 2)
+                quantise_l(c, 3, 4)
                 product(c, 3)
                 result(c, 0, "s")
                 store(c, 0, 1)
@@ -369,9 +380,9 @@ def tile_scaledconvolutionaldotproduct_pa_t_kernel(tc, qp, kp, vp, mask, out):
                 for j in range(3):
                     relu(c + 1, j)
                 scores(c + 1, 3)
-                relu(c + 1, 3)
             for n in (2, 3):
-                transposes(c + 2, n)
+                if (c, n) != (0, 2):
+                    transposes(c + 2, n)
                 copy(c + 2, n, "s")
             if c != 0:
                 clamp(c)

import math
from contextlib import ExitStack

import concourse.mybir as mybir
from concourse.masks import make_identity

F32 = mybir.dt.float32
BF16 = mybir.dt.bfloat16
U32 = mybir.dt.uint32
U8 = mybir.dt.uint8
FP8X4 = mybir.dt.float8_e4m3fn_x4
ALU = mybir.AluOpType
ACT = mybir.ActivationFunctionType

NB = 8
S = 512
D = 512
P = 128
FLOPS = 2 * 2 * NB * S * S * D

INV_SQRT_D = 1.0 / math.sqrt(D)
RELU_BANKS = (0, 0, 0, 0, 0, 0, 0, 4)
G_GROUPS = 104
V_LAST_FROM = 3


def tile_scaledconvolutionaldotproduct_pa_t_kernel(tc, qp, kp, vp, mask, out):
    nc = tc.nc
    with ExitStack() as ctx:
        ctx.enter_context(tc.manual_schedule())
        const = ctx.enter_context(tc.tile_pool(name="const", bufs=1))
        raw = ctx.enter_context(tc.tile_pool(name="raw", bufs=NB))
        work = ctx.enter_context(tc.tile_pool(name="work", bufs=2))
        ps_t = ctx.enter_context(tc.psum_pool(name="ps_t", bufs=3))
        ps_1 = ctx.enter_context(tc.psum_pool(name="ps_1", bufs=3))
        ps_2 = ctx.enter_context(tc.psum_pool(name="ps_2", bufs=2))

        ident = const.tile([P, P], F32)
        make_identity(nc, ident[:])
        m_sb = const.tile([P, 4 * S], BF16)
        mask_g = const.tile([P, 4 * S], BF16, align_bytes=64)

        st = {}

        def live(b):
            return 0 <= b < NB

        def rows(x):
            return x.rearrange("(p j) d -> p (j d)", j=4)

        def load_kq(b):
            k_sb = raw.tile([P, 4 * D], BF16)
            q_sb = raw.tile([P, 4 * D], BF16)
            if b == 0:
                for x_sb, x in ((k_sb, kp[0]), (q_sb, qp[0]), (m_sb, mask[0])):
                    for h in range(2):
                        half = slice(2 * D * h, 2 * D * (h + 1))
                        nc.sync.dma_start(out=x_sb[:, half], in_=rows(x)[:, half])
            else:
                nc.sync.dma_start(out=k_sb[:], in_=rows(kp[b]))
                nc.sync.dma_start(out=q_sb[:], in_=rows(qp[b]))
            st[("raw", b)] = (k_sb, q_sb)

        def load_v(b):
            v_sb = raw.tile([P, 4 * D], BF16)
            nc.sync.dma_start(out=v_sb[:], in_=rows(vp[b]))
            st[("v", b)] = v_sb

        def copy_out(engine, dst, src):
            if engine == "s":
                nc.scalar.copy(out=dst, in_=src)
            else:
                nc.vector.tensor_copy(out=dst, in_=src)

        def unpack(engine, g32, n, tp):
            copy_out(
                engine,
                g32[:, 512 * n : 512 * (n + 1)].rearrange("p (j r u) -> p j r u", j=2, u=2),
                tp[:].rearrange("p j u r -> p j r u"),
            )

        def mask_transposes(h):
            m32 = m_sb[:].bitcast(F32).rearrange("r (j p u) -> r j p u", j=4, u=2)
            tp = ps_2.tile([P, 2, 2, P], F32, tag="s2")
            for jj in range(2):
                for u in range(2):
                    nc.tensor.transpose(tp[:, jj, u, :], m32[:, 2 * h + jj, :, u], ident[:])
            st[("mt", h)] = tp

        def mask_copy(h, engine):
            unpack(engine, mask_g[:].bitcast(F32), h, st[("mt", h)])

        def transposes(b, n):
            if not live(b):
                return
            if n == 0:
                qk_g = work.tile([P, 8 * S], BF16, align_bytes=64)
                st[("qkg", b)] = qk_g
            s32 = st[("raw", b)][n // 2][:].bitcast(F32)
            if b == 0 and n == 3:
                tp = ps_1.tile([P, 2, 2, P], F32, tag="s1")
            else:
                tp = ps_t.tile([P, 2, 2, P], F32, tag="tp")
            for jj in range(2):
                for u in range(2):
                    c0 = (2 * (n % 2) + jj) * 256 + u
                    nc.tensor.transpose(tp[:, jj, u, :], s32[:, c0 : c0 + 255 : 2], ident[:])
            st[("tp", b, n)] = tp

        def copy(b, n, engine):
            if not live(b):
                return
            unpack(engine, st[("qkg", b)][:].bitcast(F32), n, st[("tp", b, n)])

        def quantise_qk(b, lo, hi):
            if not live(b):
                return
            if lo == 0:
                qk_c = work.tile([P, 2 * S], U32, align_bytes=64)
                qk_s = work.tile([P, 2 * S], U8, align_bytes=64)
                st[("qk", b)] = (qk_c, qk_s)
            qk_g = st[("qkg", b)]
            qk_c, qk_s = st[("qk", b)]
            w = slice(2 * P * lo, 2 * P * hi)
            nc.vector.quantize_mx(
                out=qk_c[:, w].bitcast(FP8X4),
                scales=qk_s[:, w],
                in_=qk_g[:, 8 * P * lo : 8 * P * hi],
            )

        def scores(b, j):
            if not live(b):
                return
            qk_c, qk_s = st[("qk", b)]
            if ("s1", b, j) not in st:
                s1 = ps_1.tile([P, 4, P], F32, tag="s1")
                st[("s1", b, j)] = s1
            s1 = st[("s1", b, j)]
            for t in range(4):
                kc = slice(P * t, P * (t + 1))
                qc = slice(S + P * j, S + P * (j + 1))
                nc.tensor.matmul_mx(
                    out=s1[:, t, :],
                    lhsT=qk_c[:, kc].bitcast(FP8X4),
                    lhsT_scale=qk_s[:, kc],
                    rhs=qk_c[:, qc].bitcast(FP8X4),
                    rhs_scale=qk_s[:, qc],
                    start=True,
                    stop=True,
                )

        def relu(b, j):
            a = work.tile([P, P, 4], F32, bufs=4)
            nc.scalar.activation(
                out=a[:],
                in_=st[("s1", b, j)][:].rearrange("p t r -> p r t"),
                func=ACT.Relu,
                scale=INV_SQRT_D,
            )
            st[("a", b, j)] = a

        def relu_banks(b):
            return RELU_BANKS[b] if live(b) else 0

        def logits(b, j):
            if not live(b):
                return
            cols = slice(4 * P * j, 4 * P * (j + 1))
            if j == 0:
                l_g = work.tile([P, 4 * S], BF16, align_bytes=64)
                st[("l", b)] = l_g
            if j >= 4 - RELU_BANKS[b]:
                nc.vector.tensor_tensor(
                    out=st[("l", b)][:, cols],
                    in0=st[("a", b, j)][:].rearrange("p r t -> p (r t)"),
                    in1=mask_g[:, cols],
                    op=ALU.add,
                )
                return
            if j == 0:
                x_g = work.tile([P, 4 * S], BF16, align_bytes=64)
                st[("x", b)] = x_g
            x_g = st[("x", b)]
            nc.vector.scalar_tensor_tensor(
                out=x_g[:, cols].rearrange("p (r t) -> p r t", t=4),
                in0=st[("s1", b, j)][:].rearrange("p t r -> p r t"),
                scalar=INV_SQRT_D,
                in1=mask_g[:, cols].rearrange("p (r t) -> p r t", t=4),
                op0=ALU.mult,
                op1=ALU.add,
            )

        def clamp(b):
            if not live(b) or RELU_BANKS[b] == 4:
                return
            rest = slice(0, 4 * P * (4 - RELU_BANKS[b]))
            nc.vector.tensor_tensor(
                out=st[("l", b)][:, rest], in0=st[("x", b)][:, rest], in1=mask_g[:, rest], op=ALU.max
            )

        def quantise_l(b, lo, hi):
            if not live(b):
                return
            if lo == 0:
                l_c = work.tile([P, S], U32, align_bytes=64)
                l_s = work.tile([P, S], U8, align_bytes=64)
                st[("lc", b)] = (l_c, l_s)
            l_c, l_s = st[("lc", b)]
            w = slice(P * lo, P * hi)
            nc.vector.quantize_mx(
                out=l_c[:, w].bitcast(FP8X4),
                scales=l_s[:, w],
                in_=st[("l", b)][:, 4 * P * lo : 4 * P * hi],
            )

        def regroup(b, engine, lo, hi):
            if not live(b) or lo == hi:
                return
            if ("vg", b) not in st:
                if b == NB - 1:
                    v_last = const.tile([P, 4 * D], BF16, align_bytes=64)
                    st[("vg", b)] = v_last
                else:
                    v_g = const.tile([P, 4 * D], BF16, align_bytes=64)
                    st[("vg", b)] = v_g
            dst = st[("vg", b)][:].rearrange("p (c i t) -> p c t i", i=4, t=4)[:, lo:hi]
            src = st[("v", b)][:].rearrange("p (t c i) -> p c t i", i=4, t=4)[:, lo:hi]
            if engine == "g":
                nc.gpsimd.tensor_scalar(
                    out=dst, in0=src, scalar1=1.0, scalar2=0.0, op0=ALU.mult, op1=ALU.add
                )
            else:
                copy_out(engine, dst, src)

        def gate_regroup(b):
            v_g = const.tile([P, 4 * D], BF16, align_bytes=64)
            st[("vg", b)] = v_g
            nc.vector.memset(v_g[:, :2], 0.0)

        def quantise_v(b):
            if not live(b):
                return
            v_c = work.tile([P, D], U32, align_bytes=64)
            v_s = work.tile([P, D], U8, align_bytes=64)
            nc.vector.quantize_mx(out=v_c[:].bitcast(FP8X4), scales=v_s[:], in_=st[("vg", b)][:])
            st[("vc", b)] = (v_c, v_s)

        def product(b, j, bank="2"):
            if not live(b):
                return
            l_c, l_s = st[("lc", b)]
            v_c, v_s = st[("vc", b)]
            if bank == "t":
                s2 = ps_t.tile([P, D], F32, tag="tp")
            elif bank == "1":
                s2 = ps_1.tile([P, D], F32, tag="s1")
            else:
                s2 = ps_2.tile([P, D], F32, tag="s2")
            qc = slice(P * j, P * (j + 1))
            nc.tensor.matmul_mx(
                out=s2[:],
                lhsT=l_c[:, qc].bitcast(FP8X4),
                lhsT_scale=l_s[:, qc],
                rhs=v_c[:].bitcast(FP8X4),
                rhs_scale=v_s[:],
                start=True,
                stop=True,
            )
            st[("s2", b, j)] = s2

        def result(b, j, engine):
            if not live(b):
                return
            if j == 0:
                o_sb = work.tile([P, 4 * D], F32, bufs=5)
                st[("o", b)] = o_sb
            dst = st[("o", b)][:, D * j : D * (j + 1)]
            if engine == "s":
                nc.scalar.activation(out=dst, in_=st[("s2", b, j)][:], func=ACT.Relu)
            else:
                nc.vector.tensor_scalar_max(out=dst, in0=st[("s2", b, j)][:], scalar1=0.0)

        def store(b, lo, hi):
            if not live(b):
                return
            part = slice(D * lo, D * hi)
            nc.sync.dma_start(out=rows(out[b])[:, part], in_=st[("o", b)][:, part])

        load_kq(0)
        for b in range(1, NB):
            load_v(b - 1)
            load_kq(b)
        load_v(NB - 1)

        for n in range(4):
            transposes(0, n)
        copy(0, 0, "v")
        copy(0, 1, "s")
        mask_transposes(0)
        copy(0, 2, "s")
        quantise_qk(0, 0, 2)
        copy(0, 3, "s")
        quantise_qk(0, 2, 3)
        scores(0, 0)
        scores(0, 1)
        mask_transposes(1)
        mask_copy(0, "v")
        quantise_qk(0, 3, 4)
        gate_regroup(0)
        scores(0, 2)
        mask_copy(1, "s")

        last = NB - 1
        for c in range(NB):
            if c < last:
                regroup(c, "g", 0, G_GROUPS)
            logits(c, 0)
            if relu_banks(c) < 4:
                scores(c, 3)
                for j in range(4 - relu_banks(c), 4):
                    relu(c, j)
            logits(c, 1)
            if c == 0:
                for n in range(4):
                    transposes(1, n)
                    copy(1, n, "s")
            if c < last:
                regroup(c, "s", G_GROUPS, P)
            transposes(c + 2, 0)
            transposes(c + 2, 1)
            if c == 0:
                transposes(c + 2, 2)
            result(c - 1, 0, "s")
            product(c - 1, 2, "t" if c == last else "2")
            result(c - 1, 1, "s")
            if c == last:
                relu(c, 3)
            product(c - 1, 3, "t" if c == last else "2")
            logits(c, 2)
            if c == last:
                quantise_l(c, 0, 2)
                product(c, 0, "1")
                product(c, 1, "1")
            logits(c, 3)
            copy(c + 2, 0, "s")
            copy(c + 2, 1, "s")
            if c == last:
                store(c - 1, 0, 1)
                store(c - 1, 1, 2)
            result(c - 1, 2, "s")
            if c == last:
                store(c - 1, 2, 3)
            else:
                store(c - 1, 0, 2)
            result(c - 1, 3, "s")
            store(c - 1, 3 if c == last else 2, 4)
            if c == last:
                quantise_l(c, 2, 3)
                product(c, 2)
                quantise_l(c, 3, 4)
                product(c, 3)
                result(c, 0, "s")
                store(c, 0, 1)
                result(c, 1, "v")
                store(c, 1, 2)
                result(c, 2, "s")
                store(c, 2, 3)
                result(c, 3, "v")
                store(c, 3, 4)
                break
            if c >= V_LAST_FROM:
                piece = P // (last - V_LAST_FROM)
                regroup(last, "s", piece * (c - V_LAST_FROM), piece * (c + 1 - V_LAST_FROM))
            if c == 0:
                clamp(c)
            quantise_qk(c + 1, 0, 4)
            for j in range(3):
                scores(c + 1, j)
            if relu_banks(c + 1) == 4:
                for j in range(3):
                    relu(c + 1, j)
                scores(c + 1, 3)
            for n in (2, 3):
                if (c, n) != (0, 2):
                    transposes(c + 2, n)
                copy(c + 2, n, "s")
            if c != 0:
                clamp(c)
            quantise_v(c)
            quantise_l(c, 0, 4)
            if c + 1 == last:
                quantise_v(last)
            product(c, 0)
            product(c, 1)
